import numpy as np
import ml_dtypes


def mxq(x, axis, fmt="e4m3"):
    dtype, down = {"e4m3": (ml_dtypes.float8_e4m3fn, 7), "e5m2": (ml_dtypes.float8_e5m2, 14)}[fmt]
    v = np.moveaxis(np.asarray(x, np.float32).astype(ml_dtypes.bfloat16).astype(np.float64), axis, -1)
    blocks = v.reshape(v.shape[:-1] + (-1, 32))
    amax = np.abs(blocks).max(-1, keepdims=True)
    byte = np.maximum(np.where(amax > 0, np.frexp(amax)[1] - 1 + 127, 0) - down, 1)
    scale = np.exp2(byte - 127.0)
    codes = (blocks / scale).astype(np.float32).astype(dtype).astype(np.float64)
    return np.moveaxis((codes * scale).reshape(v.shape), -1, axis)


WIDE = False


def mx_kscale(k):
    if not WIDE:
        return np.ones(k)
    levels = np.array([10, -10, 5, -5, 0])
    a = np.random.permutation(np.resize(levels, k // 512 * 4)).reshape(k // 512, 4)
    idx = np.arange(k)
    return np.exp2(a[idx // 512, idx % 128 // 32])


BF16 = ml_dtypes.bfloat16


def bf(x):
    return np.asarray(x, np.float32).astype(BF16)


def f64(x):
    return np.asarray(x).astype(np.float64)


B, S, H, HO, E = 4, 1024, 1024, 128, 8


def kahan_sum_last(x):
    s = np.zeros_like(x[..., 0])
    c = np.zeros_like(s)
    for i in range(x.shape[-1]):
        y = x[..., i] - c
        t = s + y
        c = (t - s) - y
        s = t
    return s


def setup_inputs():
    s = mx_kscale(H)
    return {"hidden_states": bf(np.random.standard_normal((B, S, H)) * s),
            "op_logits": bf(np.random.standard_normal((B, S, E)) * 1.3),
            "We": bf(np.random.standard_normal((E, H, HO)) / np.sqrt(H) / s[None, :, None]),
            "be": bf(np.random.standard_normal((E, HO)) * 0.3)}


def reference(hidden_states, op_logits, We, be):
    l = f64(op_logits)
    ex = np.exp(l - l.max(-1, keepdims=True))
    op_w = ex / ex.sum(-1, keepdims=True)
    prod = mxq(f64(hidden_states), 2, "e4m3")[:, None] @ mxq(f64(We), 1, "e4m3")[None]
    expert_out = prod.transpose(0, 2, 1, 3) + f64(be)
    weighted = expert_out * op_w[:, :, :, None]
    return kahan_sum_last(np.moveaxis(weighted, 2, -1))

@@ -1,0 +1,256 @@
+from contextlib import ExitStack
+
+import concourse.mybir as mybir
+from concourse.masks import make_identity
+
+F32 = mybir.dt.float32
+BF16 = mybir.dt.bfloat16
+U32 = mybir.dt.uint32
+U8 = mybir.dt.uint8
+FP8X4 = mybir.dt.float8_e4m3fn_x4
+ALU = mybir.AluOpType
+ACT = mybir.ActivationFunctionType
+AXIS = mybir.AxisListType
+
+P = 128
+TOKENS = 4 * 1024
+K = 1024
+EXPERTS = 8
+HO = 128
+PACK = 4
+PASSES = K // (P * PACK)
+WORD_BLOCKS = K // 2 // P
+TILES = TOKENS // P
+SWEEPS = 2
+SWEEP_EXPERTS = EXPERTS // SWEEPS
+N_SWEEP = SWEEP_EXPERTS * HO
+PAIR = 2
+PAIRS = TILES // PAIR
+PAIRS_PER_ROUND = 2
+ROUNDS = PAIRS // PAIRS_PER_ROUND
+SPLIT = 2
+BIAS_ROWS = SPLIT * EXPERTS
+BIAS_BLOCK = P // BIAS_ROWS
+BIAS_TILES = N_SWEEP // HO
+
+FLOPS = 2 * TOKENS * K * EXPERTS * HO
+
+
+def tile_enhancedmathematicalreasoning_pa_t_kernel(tc, hidden_states, op_logits, We, be, out):
+    nc = tc.nc
+    x_dram = hidden_states.flatten_outer_dims().rearrange("(p j) k -> p j k", j=TILES)
+    logit_dram = op_logits.flatten_outer_dims().rearrange("(p j) e -> p j e", j=TILES)
+    out_dram = out.flatten_outer_dims().rearrange("(p j) o -> p j o", j=TILES)
+
+    with ExitStack() as stack:
+        keep = stack.enter_context(tc.tile_pool(name="keep", bufs=1))
+        stage = stack.enter_context(tc.tile_pool(name="stage", bufs=2 * PAIRS_PER_ROUND))
+        flip_banks = stack.enter_context(tc.psum_pool(name="flip_banks", bufs=PAIR * PAIRS_PER_ROUND))
+        sum_banks = stack.enter_context(tc.psum_pool(name="sum_banks", bufs=4))
+        stack.enter_context(tc.manual_schedule())
+
+        ident_bf = keep.tile([P, P], BF16)
+        make_identity(nc, ident_bf[:])
+        ident_f32 = keep.tile([P, P], F32)
+        make_identity(nc, ident_f32[:])
+
+        logit_bf = keep.tile([P, TILES, EXPERTS], BF16)
+        nc.scalar.dma_start(out=logit_bf[:], in_=logit_dram)
+        be_rows = keep.tile([P, HO], BF16)
+        nc.vector.memset(be_rows[:], 0.0)
+        nc.scalar.dma_start(out=be_rows[0:EXPERTS, :], in_=be)
+
+        w_raw = keep.tile([P, SWEEPS, PASSES, SWEEP_EXPERTS, PACK, HO], BF16)
+
+        def load_weights(s):
+            for c in range(PASSES):
+                for u in range(2):
+                    first_row = (2 * c + u) * 2 * P
+                    nc.sync.dma_start(
+                        out=w_raw[:, s, c, :, 2 * u : 2 * u + 2, :],
+                        in_=We[
+                            s * SWEEP_EXPERTS : (s + 1) * SWEEP_EXPERTS, first_row : first_row + 2 * P, :
+                        ].rearrange("e (p i) o -> p e i o", i=2),
+                    )
+
+        x_all = keep.tile([P, TILES, K], BF16)
+
+        def load_pair(a):
+            tiles = slice(a * PAIR, (a + 1) * PAIR)
+            nc.sync.dma_start(out=x_all[:, tiles, :], in_=x_dram[:, tiles, :])
+
+        load_weights(0)
+        for a in range(PAIRS // 2):
+            load_pair(a)
+        load_weights(1)
+        for a in range(PAIRS // 2, PAIRS):
+            load_pair(a)
+
+        repeat = keep.tile([P, P // EXPERTS, EXPERTS], BF16)
+        nc.vector.tensor_copy(
+            out=repeat[:], in_=ident_bf[:, 0:EXPERTS].unsqueeze(1).to_broadcast([P, P // EXPERTS, EXPERTS])
+        )
+        be_bank = flip_banks.tile([P, HO], F32, tag="flip")
+        nc.tensor.matmul(
+            out=be_bank[:], lhsT=repeat[:].rearrange("p r e -> p (r e)"), rhs=be_rows[:], start=True, stop=True
+        )
+        own_tile = keep.tile([P, BIAS_BLOCK], F32)
+        nc.vector.tensor_reduce(
+            out=own_tile[:], in_=ident_f32[:].rearrange("p (j r) -> p j r", r=BIAS_ROWS), axis=AXIS.X, op=ALU.add
+        )
+        be_diag = keep.tile([P, BIAS_BLOCK, HO], BF16)
+
+        top = keep.tile([P, TILES], F32)
+        nc.vector.tensor_reduce(out=top[:], in_=logit_bf[:], axis=AXIS.X, op=ALU.max)
+        shifted = keep.tile([P, TILES, EXPERTS], F32)
+        nc.vector.tensor_tensor(
+            out=shifted[:],
+            in0=logit_bf[:],
+            in1=top[:].unsqueeze(2).to_broadcast([P, TILES, EXPERTS]),
+            op=ALU.subtract,
+        )
+        grown = keep.tile([P, TILES, EXPERTS], F32)
+        nc.scalar.activation(out=grown[:], in_=shifted[:], func=ACT.Exp)
+        for j in range(BIAS_BLOCK):
+            nc.scalar.activation(out=be_diag[:, j, :], in_=be_bank[:], func=ACT.Copy, scale=own_tile[:, j : j + 1])
+        total = keep.tile([P, TILES], F32)
+        nc.vector.tensor_reduce(out=total[:], in_=grown[:], axis=AXIS.X, op=ALU.add)
+        inverse = keep.tile([P, TILES], F32)
+        nc.vector.reciprocal(out=inverse[:], in_=total[:])
+        op_w = keep.tile([P, TILES, EXPERTS], F32)
+        nc.vector.tensor_tensor(
+            out=op_w[:],
+            in0=grown[:],
+            in1=inverse[:].unsqueeze(2).to_broadcast([P, TILES, EXPERTS]),
+            op=ALU.mult,
+        )
+
+        w_split = keep.tile([P, TILES, SPLIT, EXPERTS], BF16)
+        nc.vector.tensor_copy(out=w_split[:, :, 0, :], in_=op_w[:])
+        nc.vector.tensor_tensor(out=w_split[:, :, 1, :], in0=op_w[:], in1=w_split[:, :, 0, :], op=ALU.subtract)
+        w_rows_bank = flip_banks.tile([P, TILES // BIAS_BLOCK, P], BF16, tag="flip")
+        for g in range(TILES // BIAS_BLOCK):
+            nc.tensor.transpose(
+                w_rows_bank[:, g, :],
+                w_split[:, g * BIAS_BLOCK : (g + 1) * BIAS_BLOCK, :, :].rearrange("p j s e -> p (j s e)"),
+                ident_bf[:],
+            )
+        w_rows = keep.tile([P, TILES // BIAS_BLOCK, P], BF16)
+        nc.scalar.copy(out=w_rows[:], in_=w_rows_bank[:])
+
+        acc = keep.tile([P, TILES, HO], F32)
+
+        def bias_terms(q):
+            first = q * BIAS_TILES
+            in_block = first % BIAS_BLOCK
+            bias_bank = sum_banks.tile([P, BIAS_TILES, HO], F32, tag="sum")
+            nc.tensor.matmul(
+                out=bias_bank[:].rearrange("p j o -> p (j o)"),
+                lhsT=w_rows[:, first // BIAS_BLOCK, :],
+                rhs=be_diag[:, in_block : in_block + BIAS_TILES, :].rearrange("p j o -> p (j o)"),
+                start=True,
+                stop=True,
+            )
+            nc.scalar.copy(out=acc[:, first : first + BIAS_TILES, :], in_=bias_bank[:])
+
+        w_grouped = keep.tile([P, SWEEPS, PASSES, N_SWEEP, PACK], BF16, align_bytes=64)
+        w_codes = keep.tile([P, SWEEPS, PASSES, N_SWEEP], U32, align_bytes=64)
+        w_scales = keep.tile([P, SWEEPS, PASSES, N_SWEEP], U8, align_bytes=64)
+
+        def quantise_weights(s):
+            for c in range(PASSES):
+                nc.vector.quantize_mx(
+                    out=w_codes[:, s, c, :].bitcast(FP8X4),
+                    scales=w_scales[:, s, c, :],
+                    in_=w_grouped[:, s, c, :, :].rearrange("p n v -> p (n v)"),
+                )
+
+        for c in range(PASSES):
+            nc.vector.tensor_copy(
+                out=w_grouped[:, 0, c, :, :].rearrange("p (e o) v -> p e o v", e=SWEEP_EXPERTS),
+                in_=w_raw[:, 0, c, :, :, :].rearrange("p e v o -> p e o v"),
+            )
+        quantise_weights(0)
+
+        def regroup_late_expert(e):
+            for c in range(PASSES):
+                nc.scalar.copy(
+                    out=w_grouped[:, 1, c, e * HO : (e + 1) * HO, :],
+                    in_=w_raw[:, 1, c, e, :, :].rearrange("p v o -> p o v"),
+                )
+
+        x_codes = keep.tile([P, TILES, PASSES, P], U32, align_bytes=64)
+        x_scales = keep.tile([P, TILES, PASSES, P], U8, align_bytes=64)
+        x_grouped = {}
+
+        def flip_pair(a):
+            x_grouped[a] = stage.tile([P, PAIR, PASSES, P, PACK], BF16, align_bytes=64, name="x_grouped")
+            for jj in range(PAIR):
+                x_words = x_all[:, a * PAIR + jj, :].bitcast(F32)
+                flipped = flip_banks.tile([P, WORD_BLOCKS, P], F32, tag="flip")
+                for b in range(WORD_BLOCKS):
+                    nc.tensor.transpose(flipped[:, b, :], x_words[:, b * P : (b + 1) * P], ident_f32[:])
+                nc.scalar.copy(
+                    out=x_grouped[a][:, jj, :, :, :].bitcast(F32),
+                    in_=flipped[:].rearrange("p (c u) t -> p c t u", u=2),
+                )
+
+        def quantise_pair(a):
+            tiles = slice(a * PAIR, (a + 1) * PAIR)
+            nc.vector.quantize_mx(
+                out=x_codes[:, tiles, :, :].rearrange("p j c t -> p (j c t)").bitcast(FP8X4),
+                scales=x_scales[:, tiles, :, :].rearrange("p j c t -> p (j c t)"),
+                in_=x_grouped[a][:].rearrange("p j c t v -> p (j c t v)"),
+            )
+
+        def multiply_pair(s, a):
+            products = []
+            for jj in range(PAIR):
+                j = a * PAIR + jj
+                product = sum_banks.tile([P, SWEEP_EXPERTS, HO], F32, tag="sum")
+                for c in range(PASSES):
+                    nc.tensor.matmul_mx(
+                        out=product[:].rearrange("p e o -> p (e o)"),
+                        lhsT=x_codes[:, j, c, :].bitcast(FP8X4),
+                        lhsT_scale=x_scales[:, j, c, :],
+                        rhs=w_codes[:, s, c, :].bitcast(FP8X4),
+                        rhs_scale=w_scales[:, s, c, :],
+                        start=(c == 0),
+                        stop=(c == PASSES - 1),
+                    )
+                products.append(product)
+            for e in range(SWEEP_EXPERTS):
+                for jj in range(PAIR):
+                    j = a * PAIR + jj
+                    nc.vector.scalar_tensor_tensor(
+                        out=acc[:, j, :],
+                        in0=products[jj][:, e, :],
+                        scalar=op_w[:, j, s * SWEEP_EXPERTS + e : s * SWEEP_EXPERTS + e + 1],
+                        in1=acc[:, j, :],
+                        op0=ALU.mult,
+                        op1=ALU.add,
+                    )
+
+        late_start = ROUNDS - SWEEP_EXPERTS
+        for i in range(ROUNDS + 1):
+            if i < ROUNDS:
+                for n in range(PAIRS_PER_ROUND):
+                    flip_pair(i * PAIRS_PER_ROUND + n)
+                for n in range(PAIRS_PER_ROUND):
+                    first_tile = (i * PAIRS_PER_ROUND + n) * PAIR
+                    if first_tile % BIAS_TILES == 0:
+                        bias_terms(first_tile // BIAS_TILES)
+                if i >= late_start:
+                    regroup_late_expert(i - late_start)
+            else:
+                quantise_weights(1)
+            for n in range(PAIRS_PER_ROUND):
+                if i > 0:
+                    multiply_pair(0, (i - 1) * PAIRS_PER_ROUND + n)
+                if i < ROUNDS:
+                    quantise_pair(i * PAIRS_PER_ROUND + n)
+
+        for a in range(PAIRS):
+            multiply_pair(1, a)
+            tiles = slice(a * PAIR, (a + 1) * PAIR)
+            nc.sync.dma_start(out=out_dram[:, tiles, :], in_=acc[:, tiles, :])

@@ -24,14 +24,22 @@ TILES = TOKENS // P
 SWEEPS = 2
 SWEEP_EXPERTS = EXPERTS // SWEEPS
 N_SWEEP = SWEEP_EXPERTS * HO
+BANK_F32 = 512
+GROUP_EXPERTS = 2
+N_GROUP = GROUP_EXPERTS * HO
+GROUPS_PER_SWEEP = SWEEP_EXPERTS // GROUP_EXPERTS
+BANK_TILES = BANK_F32 // N_GROUP
 PAIR = 2
 PAIRS = TILES // PAIR
-PAIRS_PER_ROUND = 2
-ROUNDS = PAIRS // PAIRS_PER_ROUND
+ROUND_TILES = 4
+PAIRS_PER_ROUND = ROUND_TILES // PAIR
+ROUNDS = TILES // ROUND_TILES
 SPLIT = 2
 BIAS_ROWS = SPLIT * EXPERTS
 BIAS_BLOCK = P // BIAS_ROWS
-BIAS_TILES = N_SWEEP // HO
+BIAS_TILES = BANK_F32 // HO
+assert BIAS_TILES == ROUND_TILES
+assert PAIRS_PER_ROUND == GROUPS_PER_SWEEP
 
 FLOPS = 2 * TOKENS * K * EXPERTS * HO
 
@@ -45,8 +53,7 @@ def tile_enhancedmathematicalreasoning_pa_t_kernel(tc, hidden_states, op_logits,
     with ExitStack() as stack:
         keep = stack.enter_context(tc.tile_pool(name="keep", bufs=1))
         stage = stack.enter_context(tc.tile_pool(name="stage", bufs=2 * PAIRS_PER_ROUND))
-        flip_banks = stack.enter_context(tc.psum_pool(name="flip_banks", bufs=PAIR * PAIRS_PER_ROUND))
-        sum_banks = stack.enter_context(tc.psum_pool(name="sum_banks", bufs=4))
+        banks = stack.enter_context(tc.psum_pool(name="banks", bufs=8))
         stack.enter_context(tc.manual_schedule())
 
         ident_bf = keep.tile([P, P], BF16)
@@ -90,7 +97,7 @@ def tile_enhancedmathematicalreasoning_pa_t_kernel(tc, hidden_states, op_logits,
         nc.vector.tensor_copy(
             out=repeat[:], in_=ident_bf[:, 0:EXPERTS].unsqueeze(1).to_broadcast([P, P // EXPERTS, EXPERTS])
         )
-        be_bank = flip_banks.tile([P, HO], F32, tag="flip")
+        be_bank = banks.tile([P, HO], F32, tag="bank")
         nc.tensor.matmul(
             out=be_bank[:], lhsT=repeat[:].rearrange("p r e -> p (r e)"), rhs=be_rows[:], start=True, stop=True
         )
@@ -128,7 +135,7 @@ def tile_enhancedmathematicalreasoning_pa_t_kernel(tc, hidden_states, op_logits,
         w_split = keep.tile([P, TILES, SPLIT, EXPERTS], BF16)
         nc.vector.tensor_copy(out=w_split[:, :, 0, :], in_=op_w[:])
         nc.vector.tensor_tensor(out=w_split[:, :, 1, :], in0=op_w[:], in1=w_split[:, :, 0, :], op=ALU.subtract)
-        w_rows_bank = flip_banks.tile([P, TILES // BIAS_BLOCK, P], BF16, tag="flip")
+        w_rows_bank = banks.tile([P, TILES // BIAS_BLOCK, P], BF16, tag="bank")
         for g in range(TILES // BIAS_BLOCK):
             nc.tensor.transpose(
                 w_rows_bank[:, g, :],
@@ -143,7 +150,7 @@ def tile_enhancedmathematicalreasoning_pa_t_kernel(tc, hidden_states, op_logits,
         def bias_terms(q):
             first = q * BIAS_TILES
             in_block = first % BIAS_BLOCK
-            bias_bank = sum_banks.tile([P, BIAS_TILES, HO], F32, tag="sum")
+            bias_bank = banks.tile([P, BIAS_TILES, HO], F32, tag="bank")
             nc.tensor.matmul(
                 out=bias_bank[:].rearrange("p j o -> p (j o)"),
                 lhsT=w_rows[:, first // BIAS_BLOCK, :],
@@ -187,7 +194,7 @@ def tile_enhancedmathematicalreasoning_pa_t_kernel(tc, hidden_states, op_logits,
             x_grouped[a] = stage.tile([P, PAIR, PASSES, P, PACK], BF16, align_bytes=64, name="x_grouped")
             for jj in range(PAIR):
                 x_words = x_all[:, a * PAIR + jj, :].bitcast(F32)
-                flipped = flip_banks.tile([P, WORD_BLOCKS, P], F32, tag="flip")
+                flipped = banks.tile([P, WORD_BLOCKS, P], F32, tag="bank")
                 for b in range(WORD_BLOCKS):
                     nc.tensor.transpose(flipped[:, b, :], x_words[:, b * P : (b + 1) * P], ident_f32[:])
                 nc.scalar.copy(
@@ -203,29 +210,33 @@ def tile_enhancedmathematicalreasoning_pa_t_kernel(tc, hidden_states, op_logits,
                 in_=x_grouped[a][:].rearrange("p j c t v -> p (j c t v)"),
             )
 
-        def multiply_pair(s, a):
+        def multiply_round(g, i):
+            s, part = divmod(g, GROUPS_PER_SWEEP)
+            columns = slice(part * N_GROUP, (part + 1) * N_GROUP)
             products = []
-            for jj in range(PAIR):
-                j = a * PAIR + jj
-                product = sum_banks.tile([P, SWEEP_EXPERTS, HO], F32, tag="sum")
-                for c in range(PASSES):
-                    nc.tensor.matmul_mx(
-                        out=product[:].rearrange("p e o -> p (e o)"),
-                        lhsT=x_codes[:, j, c, :].bitcast(FP8X4),
-                        lhsT_scale=x_scales[:, j, c, :],
-                        rhs=w_codes[:, s, c, :].bitcast(FP8X4),
-                        rhs_scale=w_scales[:, s, c, :],
-                        start=(c == 0),
-                        stop=(c == PASSES - 1),
-                    )
+            for b in range(ROUND_TILES // BANK_TILES):
+                product = banks.tile([P, BANK_TILES, GROUP_EXPERTS, HO], F32, tag="bank")
+                for jj in range(BANK_TILES):
+                    j = i * ROUND_TILES + b * BANK_TILES + jj
+                    for c in range(PASSES):
+                        nc.tensor.matmul_mx(
+                            out=product[:, jj, :, :].rearrange("p e o -> p (e o)"),
+                            lhsT=x_codes[:, j, c, :].bitcast(FP8X4),
+                            lhsT_scale=x_scales[:, j, c, :],
+                            rhs=w_codes[:, s, c, columns].bitcast(FP8X4),
+                            rhs_scale=w_scales[:, s, c, columns],
+                            start=(c == 0),
+                            stop=(c == PASSES - 1),
+                        )
                 products.append(product)
-            for e in range(SWEEP_EXPERTS):
-                for jj in range(PAIR):
-                    j = a * PAIR + jj
+            for e in range(GROUP_EXPERTS):
+                expert = g * GROUP_EXPERTS + e
+                for n in range(ROUND_TILES):
+                    j = i * ROUND_TILES + n
                     nc.vector.scalar_tensor_tensor(
                         out=acc[:, j, :],
-                        in0=products[jj][:, e, :],
-                        scalar=op_w[:, j, s * SWEEP_EXPERTS + e : s * SWEEP_EXPERTS + e + 1],
+                        in0=products[n // BANK_TILES][:, n % BANK_TILES, e, :],
+                        scalar=op_w[:, j, expert : expert + 1],
                         in1=acc[:, j, :],
                         op0=ALU.mult,
                         op1=ALU.add,
@@ -236,21 +247,19 @@ def tile_enhancedmathematicalreasoning_pa_t_kernel(tc, hidden_states, op_logits,
             if i < ROUNDS:
                 for n in range(PAIRS_PER_ROUND):
                     flip_pair(i * PAIRS_PER_ROUND + n)
-                for n in range(PAIRS_PER_ROUND):
-                    first_tile = (i * PAIRS_PER_ROUND + n) * PAIR
-                    if first_tile % BIAS_TILES == 0:
-                        bias_terms(first_tile // BIAS_TILES)
+                bias_terms(i)
                 if i >= late_start:
                     regroup_late_expert(i - late_start)
             else:
                 quantise_weights(1)
-            for n in range(PAIRS_PER_ROUND):
+            for g in range(GROUPS_PER_SWEEP):
                 if i > 0:
-                    multiply_pair(0, (i - 1) * PAIRS_PER_ROUND + n)
+                    multiply_round(g, i - 1)
                 if i < ROUNDS:
-                    quantise_pair(i * PAIRS_PER_ROUND + n)
+                    quantise_pair(i * PAIRS_PER_ROUND + g)
 
-        for a in range(PAIRS):
-            multiply_pair(1, a)
-            tiles = slice(a * PAIR, (a + 1) * PAIR)
+        for i in range(ROUNDS):
+            for g in range(GROUPS_PER_SWEEP, 2 * GROUPS_PER_SWEEP):
+                multiply_round(g, i)
+            tiles = slice(i * ROUND_TILES, (i + 1) * ROUND_TILES)
             nc.sync.dma_start(out=out_dram[:, tiles, :], in_=acc[:, tiles, :])

@@ -210,37 +210,53 @@ def tile_enhancedmathematicalreasoning_pa_t_kernel(tc, hidden_states, op_logits,
                 in_=x_grouped[a][:].rearrange("p j c t v -> p (j c t v)"),
             )
 
-        def multiply_round(g, i):
-            s, part = divmod(g, GROUPS_PER_SWEEP)
-            columns = slice(part * N_GROUP, (part + 1) * N_GROUP)
+        def add_weighted(product, expert, j):
+            nc.vector.scalar_tensor_tensor(
+                out=acc[:, j, :],
+                in0=product,
+                scalar=op_w[:, j, expert : expert + 1],
+                in1=acc[:, j, :],
+                op0=ALU.mult,
+                op1=ALU.add,
+            )
+
+        def multiply(product, j, first_expert, experts):
+            s, e = divmod(first_expert, SWEEP_EXPERTS)
+            columns = slice(e * HO, (e + experts) * HO)
+            for c in range(PASSES):
+                nc.tensor.matmul_mx(
+                    out=product,
+                    lhsT=x_codes[:, j, c, :].bitcast(FP8X4),
+                    lhsT_scale=x_scales[:, j, c, :],
+                    rhs=w_codes[:, s, c, columns].bitcast(FP8X4),
+                    rhs_scale=w_scales[:, s, c, columns],
+                    start=(c == 0),
+                    stop=(c == PASSES - 1),
+                )
+
+        def two_experts(first_expert, i):
             products = []
             for b in range(ROUND_TILES // BANK_TILES):
                 product = banks.tile([P, BANK_TILES, GROUP_EXPERTS, HO], F32, tag="bank")
                 for jj in range(BANK_TILES):
-                    j = i * ROUND_TILES + b * BANK_TILES + jj
-                    for c in range(PASSES):
-                        nc.tensor.matmul_mx(
-                            out=product[:, jj, :, :].rearrange("p e o -> p (e o)"),
-                            lhsT=x_codes[:, j, c, :].bitcast(FP8X4),
-                            lhsT_scale=x_scales[:, j, c, :],
-                            rhs=w_codes[:, s, c, columns].bitcast(FP8X4),
-                            rhs_scale=w_scales[:, s, c, columns],
-                            start=(c == 0),
-                            stop=(c == PASSES - 1),
-                        )
+                    multiply(
+                        product[:, jj, :, :].rearrange("p e o -> p (e o)"),
+                        i * ROUND_TILES + b * BANK_TILES + jj,
+                        first_expert,
+                        GROUP_EXPERTS,
+                    )
                 products.append(product)
             for e in range(GROUP_EXPERTS):
-                expert = g * GROUP_EXPERTS + e
                 for n in range(ROUND_TILES):
-                    j = i * ROUND_TILES + n
-                    nc.vector.scalar_tensor_tensor(
-                        out=acc[:, j, :],
-                        in0=products[n // BANK_TILES][:, n % BANK_TILES, e, :],
-                        scalar=op_w[:, j, expert : expert + 1],
-                        in1=acc[:, j, :],
-                        op0=ALU.mult,
-                        op1=ALU.add,
+                    add_weighted(
+                        products[n // BANK_TILES][:, n % BANK_TILES, e, :], first_expert + e, i * ROUND_TILES + n
                     )
+
+        def one_expert(expert, i):
+            product = banks.tile([P, ROUND_TILES, HO], F32, tag="bank")
+            for n in range(ROUND_TILES):
+                multiply(product[:, n, :], i * ROUND_TILES + n, expert, 1)
+            return product
 
         late_start = ROUNDS - SWEEP_EXPERTS
         for i in range(ROUNDS + 1):
@@ -254,12 +270,24 @@ def tile_enhancedmathematicalreasoning_pa_t_kernel(tc, hidden_states, op_logits,
                 quantise_weights(1)
             for g in range(GROUPS_PER_SWEEP):
                 if i > 0:
-                    multiply_round(g, i - 1)
+                    two_experts(g * GROUP_EXPERTS, i - 1)
                 if i < ROUNDS:
                     quantise_pair(i * PAIRS_PER_ROUND + g)
 
         for i in range(ROUNDS):
-            for g in range(GROUPS_PER_SWEEP, 2 * GROUPS_PER_SWEEP):
-                multiply_round(g, i)
             tiles = slice(i * ROUND_TILES, (i + 1) * ROUND_TILES)
-            nc.sync.dma_start(out=out_dram[:, tiles, :], in_=acc[:, tiles, :])
+            two_experts(SWEEP_EXPERTS, i)
+            last_product = one_expert(EXPERTS - 1, i)
+            last_term = stage.tile([P, ROUND_TILES, HO], F32)
+            for n in range(ROUND_TILES):
+                nc.scalar.activation(
+                    out=last_term[:, n, :],
+                    in_=last_product[:, n, :],
+                    func=ACT.Copy,
+                    scale=op_w[:, i * ROUND_TILES + n, EXPERTS - 1 : EXPERTS],
+                )
+            product = one_expert(EXPERTS - 2, i)
+            for n in range(ROUND_TILES):
+                add_weighted(product[:, n, :], EXPERTS - 2, i * ROUND_TILES + n)
+            nc.gpsimd.tensor_tensor(out=last_term[:], in0=last_term[:], in1=acc[:, tiles, :], op=ALU.add)
+            nc.sync.dma_start(out=out_dram[:, tiles, :], in_=last_term[:])

@@ -21,13 +21,10 @@ PACK = 4
 PASSES = K // (P * PACK)
 WORD_BLOCKS = K // 2 // P
 TILES = TOKENS // P
-SWEEPS = 2
-SWEEP_EXPERTS = EXPERTS // SWEEPS
-N_SWEEP = SWEEP_EXPERTS * HO
 BANK_F32 = 512
 GROUP_EXPERTS = 2
+GROUPS = EXPERTS // GROUP_EXPERTS
 N_GROUP = GROUP_EXPERTS * HO
-GROUPS_PER_SWEEP = SWEEP_EXPERTS // GROUP_EXPERTS
 BANK_TILES = BANK_F32 // N_GROUP
 PAIR = 2
 PAIRS = TILES // PAIR
@@ -39,7 +36,6 @@ BIAS_ROWS = SPLIT * EXPERTS
 BIAS_BLOCK = P // BIAS_ROWS
 BIAS_TILES = BANK_F32 // HO
 assert BIAS_TILES == ROUND_TILES
-assert PAIRS_PER_ROUND == GROUPS_PER_SWEEP
 
 FLOPS = 2 * TOKENS * K * EXPERTS * HO
 
@@ -67,16 +63,16 @@ def tile_enhancedmathematicalreasoning_pa_t_kernel(tc, hidden_states, op_logits,
         nc.vector.memset(be_rows[:], 0.0)
         nc.scalar.dma_start(out=be_rows[0:EXPERTS, :], in_=be)
 
-        w_raw = keep.tile([P, SWEEPS, PASSES, SWEEP_EXPERTS, PACK, HO], BF16)
+        w_raw = keep.tile([P, GROUPS, PASSES, GROUP_EXPERTS, PACK, HO], BF16)
 
-        def load_weights(s):
+        def load_weights(g):
             for c in range(PASSES):
                 for u in range(2):
                     first_row = (2 * c + u) * 2 * P
                     nc.sync.dma_start(
-                        out=w_raw[:, s, c, :, 2 * u : 2 * u + 2, :],
+                        out=w_raw[:, g, c, :, 2 * u : 2 * u + 2, :],
                         in_=We[
-                            s * SWEEP_EXPERTS : (s + 1) * SWEEP_EXPERTS, first_row : first_row + 2 * P, :
+                            g * GROUP_EXPERTS : (g + 1) * GROUP_EXPERTS, first_row : first_row + 2 * P, :
                         ].rearrange("e (p i) o -> p e i o", i=2),
                     )
 
@@ -92,6 +88,8 @@ def tile_enhancedmathematicalreasoning_pa_t_kernel(tc, hidden_states, op_logits,
         load_weights(1)
         for a in range(PAIRS // 2, PAIRS):
             load_pair(a)
+        for g in range(2, GROUPS):
+            load_weights(g)
 
         repeat = keep.tile([P, P // EXPERTS, EXPERTS], BF16)
         nc.vector.tensor_copy(
@@ -160,31 +158,25 @@ def tile_enhancedmathematicalreasoning_pa_t_kernel(tc, hidden_states, op_logits,
             )
             nc.scalar.copy(out=acc[:, first : first + BIAS_TILES, :], in_=bias_bank[:])
 
-        w_grouped = keep.tile([P, SWEEPS, PASSES, N_SWEEP, PACK], BF16, align_bytes=64)
-        w_codes = keep.tile([P, SWEEPS, PASSES, N_SWEEP], U32, align_bytes=64)
-        w_scales = keep.tile([P, SWEEPS, PASSES, N_SWEEP], U8, align_bytes=64)
+        w_grouped = keep.tile([P, GROUPS, PASSES, N_GROUP, PACK], BF16, align_bytes=64)
+        w_codes = keep.tile([P, GROUPS, PASSES, N_GROUP], U32, align_bytes=64)
+        w_scales = keep.tile([P, GROUPS, PASSES, N_GROUP], U8, align_bytes=64)
 
-        def quantise_weights(s):
-            for c in range(PASSES):
-                nc.vector.quantize_mx(
-                    out=w_codes[:, s, c, :].bitcast(FP8X4),
-                    scales=w_scales[:, s, c, :],
-                    in_=w_grouped[:, s, c, :, :].rearrange("p n v -> p (n v)"),
-                )
-
-        for c in range(PASSES):
-            nc.vector.tensor_copy(
-                out=w_grouped[:, 0, c, :, :].rearrange("p (e o) v -> p e o v", e=SWEEP_EXPERTS),
-                in_=w_raw[:, 0, c, :, :, :].rearrange("p e v o -> p e o v"),
+        def regroup_weights(copy, g):
+            copy(
+                out=w_grouped[:, g, :, :, :].rearrange("p c (e o) v -> p (c e) o v", e=GROUP_EXPERTS),
+                in_=w_raw[:, g, :, :, :, :].rearrange("p c e v o -> p (c e) o v"),
             )
-        quantise_weights(0)
 
-        def regroup_late_expert(e):
-            for c in range(PASSES):
-                nc.scalar.copy(
-                    out=w_grouped[:, 1, c, e * HO : (e + 1) * HO, :],
-                    in_=w_raw[:, 1, c, e, :, :].rearrange("p v o -> p o v"),
-                )
+        def quantise_weights(g):
+            nc.vector.quantize_mx(
+                out=w_codes[:, g, :, :].rearrange("p c n -> p (c n)").bitcast(FP8X4),
+                scales=w_scales[:, g, :, :].rearrange("p c n -> p (c n)"),
+                in_=w_grouped[:, g, :, :, :].rearrange("p c n v -> p (c n v)"),
+            )
+
+        regroup_weights(nc.vector.tensor_copy, 0)
+        quantise_weights(0)
 
         x_codes = keep.tile([P, TILES, PASSES, P], U32, align_bytes=64)
         x_scales = keep.tile([P, TILES, PASSES, P], U8, align_bytes=64)
@@ -210,84 +202,57 @@ def tile_enhancedmathematicalreasoning_pa_t_kernel(tc, hidden_states, op_logits,
                 in_=x_grouped[a][:].rearrange("p j c t v -> p (j c t v)"),
             )
 
-        def add_weighted(product, expert, j):
-            nc.vector.scalar_tensor_tensor(
-                out=acc[:, j, :],
-                in0=product,
-                scalar=op_w[:, j, expert : expert + 1],
-                in1=acc[:, j, :],
-                op0=ALU.mult,
-                op1=ALU.add,
-            )
-
-        def multiply(product, j, first_expert, experts):
-            s, e = divmod(first_expert, SWEEP_EXPERTS)
-            columns = slice(e * HO, (e + experts) * HO)
-            for c in range(PASSES):
-                nc.tensor.matmul_mx(
-                    out=product,
-                    lhsT=x_codes[:, j, c, :].bitcast(FP8X4),
-                    lhsT_scale=x_scales[:, j, c, :],
-                    rhs=w_codes[:, s, c, columns].bitcast(FP8X4),
-                    rhs_scale=w_scales[:, s, c, columns],
-                    start=(c == 0),
-                    stop=(c == PASSES - 1),
-                )
-
-        def two_experts(first_expert, i):
+        def multiply_round(g, i):
             products = []
             for b in range(ROUND_TILES // BANK_TILES):
                 product = banks.tile([P, BANK_TILES, GROUP_EXPERTS, HO], F32, tag="bank")
                 for jj in range(BANK_TILES):
-                    multiply(
-                        product[:, jj, :, :].rearrange("p e o -> p (e o)"),
-                        i * ROUND_TILES + b * BANK_TILES + jj,
-                        first_expert,
-                        GROUP_EXPERTS,
-                    )
+                    j = i * ROUND_TILES + b * BANK_TILES + jj
+                    for c in range(PASSES):
+                        nc.tensor.matmul_mx(
+                            out=product[:, jj, :, :].rearrange("p e o -> p (e o)"),
+                            lhsT=x_codes[:, j, c, :].bitcast(FP8X4),
+                            lhsT_scale=x_scales[:, j, c, :],
+                            rhs=w_codes[:, g, c, :].bitcast(FP8X4),
+                            rhs_scale=w_scales[:, g, c, :],
+                            start=(c == 0),
+                            stop=(c == PASSES - 1),
+                        )
                 products.append(product)
             for e in range(GROUP_EXPERTS):
+                expert = g * GROUP_EXPERTS + e
                 for n in range(ROUND_TILES):
-                    add_weighted(
-                        products[n // BANK_TILES][:, n % BANK_TILES, e, :], first_expert + e, i * ROUND_TILES + n
+                    j = i * ROUND_TILES + n
+                    nc.vector.scalar_tensor_tensor(
+                        out=acc[:, j, :],
+                        in0=products[n // BANK_TILES][:, n % BANK_TILES, e, :],
+                        scalar=op_w[:, j, expert : expert + 1],
+                        in1=acc[:, j, :],
+                        op0=ALU.mult,
+                        op1=ALU.add,
                     )
 
-        def one_expert(expert, i):
-            product = banks.tile([P, ROUND_TILES, HO], F32, tag="bank")
-            for n in range(ROUND_TILES):
-                multiply(product[:, n, :], i * ROUND_TILES + n, expert, 1)
-            return product
-
-        late_start = ROUNDS - SWEEP_EXPERTS
         for i in range(ROUNDS + 1):
+            if i == ROUNDS // 2:
+                regroup_weights(nc.vector.tensor_copy, 1)
             if i < ROUNDS:
                 for n in range(PAIRS_PER_ROUND):
                     flip_pair(i * PAIRS_PER_ROUND + n)
                 bias_terms(i)
-                if i >= late_start:
-                    regroup_late_expert(i - late_start)
-            else:
+                for n in range(PAIRS_PER_ROUND):
+                    quantise_pair(i * PAIRS_PER_ROUND + n)
+            if i == ROUNDS // 2:
                 quantise_weights(1)
-            for g in range(GROUPS_PER_SWEEP):
-                if i > 0:
-                    two_experts(g * GROUP_EXPERTS, i - 1)
-                if i < ROUNDS:
-                    quantise_pair(i * PAIRS_PER_ROUND + g)
+            if i > 0:
+                multiply_round(0, i - 1)
 
-        for i in range(ROUNDS):
-            tiles = slice(i * ROUND_TILES, (i + 1) * ROUND_TILES)
-            two_experts(SWEEP_EXPERTS, i)
-            last_product = one_expert(EXPERTS - 1, i)
-            last_term = stage.tile([P, ROUND_TILES, HO], F32)
-            for n in range(ROUND_TILES):
-                nc.scalar.activation(
-                    out=last_term[:, n, :],
-                    in_=last_product[:, n, :],
-                    func=ACT.Copy,
-                    scale=op_w[:, i * ROUND_TILES + n, EXPERTS - 1 : EXPERTS],
-                )
-            product = one_expert(EXPERTS - 2, i)
-            for n in range(ROUND_TILES):
-                add_weighted(product[:, n, :], EXPERTS - 2, i * ROUND_TILES + n)
-            nc.gpsimd.tensor_tensor(out=last_term[:], in0=last_term[:], in1=acc[:, tiles, :], op=ALU.add)
-            nc.sync.dma_start(out=out_dram[:, tiles, :], in_=last_term[:])
+        for g in range(1, GROUPS):
+            if g + 1 < GROUPS:
+                regroup_weights(nc.scalar.copy, g + 1)
+            for i in range(ROUNDS):
+                if i == ROUNDS // 2 and g + 1 < GROUPS:
+                    quantise_weights(g + 1)
+                multiply_round(g, i)
+                if g == GROUPS - 1:
+                    tiles = slice(i * ROUND_TILES, (i + 1) * ROUND_TILES)
+                    nc.sync.dma_start(out=out_dram[:, tiles, :], in_=acc[:, tiles, :])

@@ -50,7 +50,6 @@ def tile_enhancedmathematicalreasoning_pa_t_kernel(tc, hidden_states, op_logits,
         keep = stack.enter_context(tc.tile_pool(name="keep", bufs=1))
         stage = stack.enter_context(tc.tile_pool(name="stage", bufs=2 * PAIRS_PER_ROUND))
         banks = stack.enter_context(tc.psum_pool(name="banks", bufs=8))
-        stack.enter_context(tc.manual_schedule())
 
         ident_bf = keep.tile([P, P], BF16)
         make_identity(nc, ident_bf[:])

@@ -50,6 +50,7 @@ def tile_enhancedmathematicalreasoning_pa_t_kernel(tc, hidden_states, op_logits,
         keep = stack.enter_context(tc.tile_pool(name="keep", bufs=1))
         stage = stack.enter_context(tc.tile_pool(name="stage", bufs=2 * PAIRS_PER_ROUND))
         banks = stack.enter_context(tc.psum_pool(name="banks", bufs=8))
+        stack.enter_context(tc.manual_schedule())
 
         ident_bf = keep.tile([P, P], BF16)
         make_identity(nc, ident_bf[:])
@@ -57,10 +58,10 @@ def tile_enhancedmathematicalreasoning_pa_t_kernel(tc, hidden_states, op_logits,
         make_identity(nc, ident_f32[:])
 
         logit_bf = keep.tile([P, TILES, EXPERTS], BF16)
-        nc.scalar.dma_start(out=logit_bf[:], in_=logit_dram)
+        nc.sync.dma_start(out=logit_bf[:], in_=logit_dram)
         be_rows = keep.tile([P, HO], BF16)
         nc.vector.memset(be_rows[:], 0.0)
-        nc.scalar.dma_start(out=be_rows[0:EXPERTS, :], in_=be)
+        nc.sync.dma_start(out=be_rows[0:EXPERTS, :], in_=be)
 
         w_raw = keep.tile([P, GROUPS, PASSES, GROUP_EXPERTS, PACK, HO], BF16)
 

from contextlib import ExitStack

import concourse.mybir as mybir
from concourse.masks import make_identity

F32 = mybir.dt.float32
BF16 = mybir.dt.bfloat16
U32 = mybir.dt.uint32
U8 = mybir.dt.uint8
FP8X4 = mybir.dt.float8_e4m3fn_x4
ALU = mybir.AluOpType
ACT = mybir.ActivationFunctionType
AXIS = mybir.AxisListType

P = 128
TOKENS = 4 * 1024
K = 1024
EXPERTS = 8
HO = 128
PACK = 4
PASSES = K // (P * PACK)
WORD_BLOCKS = K // 2 // P
TILES = TOKENS // P
BANK_F32 = 512
GROUP_EXPERTS = 2
GROUPS = EXPERTS // GROUP_EXPERTS
N_GROUP = GROUP_EXPERTS * HO
BANK_TILES = BANK_F32 // N_GROUP
PAIR = 2
PAIRS = TILES // PAIR
ROUND_TILES = 4
PAIRS_PER_ROUND = ROUND_TILES // PAIR
ROUNDS = TILES // ROUND_TILES
SPLIT = 2
BIAS_ROWS = SPLIT * EXPERTS
BIAS_BLOCK = P // BIAS_ROWS
BIAS_TILES = BANK_F32 // HO
assert BIAS_TILES == ROUND_TILES

FLOPS = 2 * TOKENS * K * EXPERTS * HO


def tile_enhancedmathematicalreasoning_pa_t_kernel(tc, hidden_states, op_logits, We, be, out):
    nc = tc.nc
    x_dram = hidden_states.flatten_outer_dims().rearrange("(p j) k -> p j k", j=TILES)
    logit_dram = op_logits.flatten_outer_dims().rearrange("(p j) e -> p j e", j=TILES)
    out_dram = out.flatten_outer_dims().rearrange("(p j) o -> p j o", j=TILES)

    with ExitStack() as stack:
        keep = stack.enter_context(tc.tile_pool(name="keep", bufs=1))
        stage = stack.enter_context(tc.tile_pool(name="stage", bufs=2 * PAIRS_PER_ROUND))
        banks = stack.enter_context(tc.psum_pool(name="banks", bufs=8))
        stack.enter_context(tc.manual_schedule())

        ident_bf = keep.tile([P, P], BF16)
        make_identity(nc, ident_bf[:])
        ident_f32 = keep.tile([P, P], F32)
        make_identity(nc, ident_f32[:])

        logit_bf = keep.tile([P, TILES, EXPERTS], BF16)
        nc.sync.dma_start(out=logit_bf[:], in_=logit_dram)
        be_rows = keep.tile([P, HO], BF16)
        nc.vector.memset(be_rows[:], 0.0)
        nc.sync.dma_start(out=be_rows[0:EXPERTS, :], in_=be)

        w_raw = keep.tile([P, GROUPS, PASSES, GROUP_EXPERTS, PACK, HO], BF16)

        def load_weights(g):
            for c in range(PASSES):
                for u in range(2):
                    first_row = (2 * c + u) * 2 * P
                    nc.sync.dma_start(
                        out=w_raw[:, g, c, :, 2 * u : 2 * u + 2, :],
                        in_=We[
                            g * GROUP_EXPERTS : (g + 1) * GROUP_EXPERTS, first_row : first_row + 2 * P, :
                        ].rearrange("e (p i) o -> p e i o", i=2),
                    )

        x_all = keep.tile([P, TILES, K], BF16)

        def load_pair(a):
            tiles = slice(a * PAIR, (a + 1) * PAIR)
            nc.sync.dma_start(out=x_all[:, tiles, :], in_=x_dram[:, tiles, :])

        load_weights(0)
        for a in range(PAIRS // 2):
            load_pair(a)
        load_weights(1)
        for a in range(PAIRS // 2, PAIRS):
            load_pair(a)
        for g in range(2, GROUPS):
            load_weights(g)

        repeat = keep.tile([P, P // EXPERTS, EXPERTS], BF16)
        nc.vector.tensor_copy(
            out=repeat[:], in_=ident_bf[:, 0:EXPERTS].unsqueeze(1).to_broadcast([P, P // EXPERTS, EXPERTS])
        )
        be_bank = banks.tile([P, HO], F32, tag="bank")
        nc.tensor.matmul(
            out=be_bank[:], lhsT=repeat[:].rearrange("p r e -> p (r e)"), rhs=be_rows[:], start=True, stop=True
        )
        own_tile = keep.tile([P, BIAS_BLOCK], F32)
        nc.vector.tensor_reduce(
            out=own_tile[:], in_=ident_f32[:].rearrange("p (j r) -> p j r", r=BIAS_ROWS), axis=AXIS.X, op=ALU.add
        )
        be_diag = keep.tile([P, BIAS_BLOCK, HO], BF16)

        top = keep.tile([P, TILES], F32)
        nc.vector.tensor_reduce(out=top[:], in_=logit_bf[:], axis=AXIS.X, op=ALU.max)
        shifted = keep.tile([P, TILES, EXPERTS], F32)
        nc.vector.tensor_tensor(
            out=shifted[:],
            in0=logit_bf[:],
            in1=top[:].unsqueeze(2).to_broadcast([P, TILES, EXPERTS]),
            op=ALU.subtract,
        )
        grown = keep.tile([P, TILES, EXPERTS], F32)
        nc.scalar.activation(out=grown[:], in_=shifted[:], func=ACT.Exp)
        for j in range(BIAS_BLOCK):
            nc.scalar.activation(out=be_diag[:, j, :], in_=be_bank[:], func=ACT.Copy, scale=own_tile[:, j : j + 1])
        total = keep.tile([P, TILES], F32)
        nc.vector.tensor_reduce(out=total[:], in_=grown[:], axis=AXIS.X, op=ALU.add)
        inverse = keep.tile([P, TILES], F32)
        nc.vector.reciprocal(out=inverse[:], in_=total[:])
        op_w = keep.tile([P, TILES, EXPERTS], F32)
        nc.vector.tensor_tensor(
            out=op_w[:],
            in0=grown[:],
            in1=inverse[:].unsqueeze(2).to_broadcast([P, TILES, EXPERTS]),
            op=ALU.mult,
        )

        w_split = keep.tile([P, TILES, SPLIT, EXPERTS], BF16)
        nc.vector.tensor_copy(out=w_split[:, :, 0, :], in_=op_w[:])
        nc.vector.tensor_tensor(out=w_split[:, :, 1, :], in0=op_w[:], in1=w_split[:, :, 0, :], op=ALU.subtract)
        w_rows_bank = banks.tile([P, TILES // BIAS_BLOCK, P], BF16, tag="bank")
        for g in range(TILES // BIAS_BLOCK):
            nc.tensor.transpose(
                w_rows_bank[:, g, :],
                w_split[:, g * BIAS_BLOCK : (g + 1) * BIAS_BLOCK, :, :].rearrange("p j s e -> p (j s e)"),
                ident_bf[:],
            )
        w_rows = keep.tile([P, TILES // BIAS_BLOCK, P], BF16)
        nc.scalar.copy(out=w_rows[:], in_=w_rows_bank[:])

        acc = keep.tile([P, TILES, HO], F32)

        def bias_terms(q):
            first = q * BIAS_TILES
            in_block = first % BIAS_BLOCK
            bias_bank = banks.tile([P, BIAS_TILES, HO], F32, tag="bank")
            nc.tensor.matmul(
                out=bias_bank[:].rearrange("p j o -> p (j o)"),
                lhsT=w_rows[:, first // BIAS_BLOCK, :],
                rhs=be_diag[:, in_block : in_block + BIAS_TILES, :].rearrange("p j o -> p (j o)"),
                start=True,
                stop=True,
            )
            nc.scalar.copy(out=acc[:, first : first + BIAS_TILES, :], in_=bias_bank[:])

        w_grouped = keep.tile([P, GROUPS, PASSES, N_GROUP, PACK], BF16, align_bytes=64)
        w_codes = keep.tile([P, GROUPS, PASSES, N_GROUP], U32, align_bytes=64)
        w_scales = keep.tile([P, GROUPS, PASSES, N_GROUP], U8, align_bytes=64)

        def regroup_weights(copy, g):
            copy(
                out=w_grouped[:, g, :, :, :].rearrange("p c (e o) v -> p (c e) o v", e=GROUP_EXPERTS),
                in_=w_raw[:, g, :, :, :, :].rearrange("p c e v o -> p (c e) o v"),
            )

        def quantise_weights(g):
            nc.vector.quantize_mx(
                out=w_codes[:, g, :, :].rearrange("p c n -> p (c n)").bitcast(FP8X4),
                scales=w_scales[:, g, :, :].rearrange("p c n -> p (c n)"),
                in_=w_grouped[:, g, :, :, :].rearrange("p c n v -> p (c n v)"),
            )

        regroup_weights(nc.vector.tensor_copy, 0)
        quantise_weights(0)

        x_codes = keep.tile([P, TILES, PASSES, P], U32, align_bytes=64)
        x_scales = keep.tile([P, TILES, PASSES, P], U8, align_bytes=64)
        x_grouped = {}

        def flip_pair(a):
            x_grouped[a] = stage.tile([P, PAIR, PASSES, P, PACK], BF16, align_bytes=64, name="x_grouped")
            for jj in range(PAIR):
                x_words = x_all[:, a * PAIR + jj, :].bitcast(F32)
                flipped = banks.tile([P, WORD_BLOCKS, P], F32, tag="bank")
                for b in range(WORD_BLOCKS):
                    nc.tensor.transpose(flipped[:, b, :], x_words[:, b * P : (b + 1) * P], ident_f32[:])
                nc.scalar.copy(
                    out=x_grouped[a][:, jj, :, :, :].bitcast(F32),
                    in_=flipped[:].rearrange("p (c u) t -> p c t u", u=2),
                )

        def quantise_pair(a):
            tiles = slice(a * PAIR, (a + 1) * PAIR)
            nc.vector.quantize_mx(
                out=x_codes[:, tiles, :, :].rearrange("p j c t -> p (j c t)").bitcast(FP8X4),
                scales=x_scales[:, tiles, :, :].rearrange("p j c t -> p (j c t)"),
                in_=x_grouped[a][:].rearrange("p j c t v -> p (j c t v)"),
            )

        def multiply_round(g, i):
            products = []
            for b in range(ROUND_TILES // BANK_TILES):
                product = banks.tile([P, BANK_TILES, GROUP_EXPERTS, HO], F32, tag="bank")
                for jj in range(BANK_TILES):
                    j = i * ROUND_TILES + b * BANK_TILES + jj
                    for c in range(PASSES):
                        nc.tensor.matmul_mx(
                            out=product[:, jj, :, :].rearrange("p e o -> p (e o)"),
                            lhsT=x_codes[:, j, c, :].bitcast(FP8X4),
                            lhsT_scale=x_scales[:, j, c, :],
                            rhs=w_codes[:, g, c, :].bitcast(FP8X4),
                            rhs_scale=w_scales[:, g, c, :],
                            start=(c == 0),
                            stop=(c == PASSES - 1),
                        )
                products.append(product)
            for e in range(GROUP_EXPERTS):
                expert = g * GROUP_EXPERTS + e
                for n in range(ROUND_TILES):
                    j = i * ROUND_TILES + n
                    nc.vector.scalar_tensor_tensor(
                        out=acc[:, j, :],
                        in0=products[n // BANK_TILES][:, n % BANK_TILES, e, :],
                        scalar=op_w[:, j, expert : expert + 1],
                        in1=acc[:, j, :],
                        op0=ALU.mult,
                        op1=ALU.add,
                    )

        for i in range(ROUNDS + 1):
            if i == ROUNDS // 2:
                regroup_weights(nc.vector.tensor_copy, 1)
            if i < ROUNDS:
                for n in range(PAIRS_PER_ROUND):
                    flip_pair(i * PAIRS_PER_ROUND + n)
                bias_terms(i)
                for n in range(PAIRS_PER_ROUND):
                    quantise_pair(i * PAIRS_PER_ROUND + n)
            if i == ROUNDS // 2:
                quantise_weights(1)
            if i > 0:
                multiply_round(0, i - 1)

        for g in range(1, GROUPS):
            if g + 1 < GROUPS:
                regroup_weights(nc.scalar.copy, g + 1)
            for i in range(ROUNDS):
                if i == ROUNDS // 2 and g + 1 < GROUPS:
                    quantise_weights(g + 1)
                multiply_round(g, i)
                if g == GROUPS - 1:
                    tiles = slice(i * ROUND_TILES, (i + 1) * ROUND_TILES)
                    nc.sync.dma_start(out=out_dram[:, tiles, :], in_=acc[:, tiles, :])
